import numpy as np
import ml_dtypes

BF16 = ml_dtypes.bfloat16


def bf(x):
    return np.asarray(x, np.float32).astype(BF16)


def f32(x):
    return np.asarray(x, np.float32)


def f64(x):
    return np.asarray(x).astype(np.float64)


def striped(idx):
    return np.tile(idx.reshape(-1, 16).T, (8, 1))


S, D, H, N = 2048, 128, 256, 1024


def setup_inputs():
    return {"table": bf(np.random.standard_normal((D, S))), "w0": bf(np.random.standard_normal((D, H)) / np.sqrt(D)), "b0": f32(0.1 * np.random.standard_normal((H, 1))), "w1": bf(np.random.standard_normal((H, H)) * np.sqrt(2.0 / H)), "b1": f32(0.1 * np.random.standard_normal((H, 1))), "w2": bf(np.random.standard_normal((H, H)) * np.sqrt(2.0 / H)), "b2": f32(0.1 * np.random.standard_normal((H, 1))), "offs": striped(np.random.permutation(np.tile(np.arange(S), 2))[:N])}


def reference(table, w0, b0, w1, b1, w2, b2, offs):
    idx = offs[:16].T.reshape(-1)
    h0 = np.maximum(f64(w0).T @ f64(table)[:, idx] + f64(b0), 0.0)
    h1 = np.maximum(f64(w1).T @ h0 + f64(b1), 0.0)
    h2 = np.maximum(f64(w2).T @ h1 + f64(b2), 0.0)
    return np.concatenate([h0, h1, h2], axis=0)

@@ -1,0 +1,82 @@
+import concourse.mybir as mybir
+
+P = 128
+S = 2048
+H = 256
+N = 1024
+LAYERS = 3
+BLOCKS = H // P
+PIECE = 512
+PIECES = N // PIECE
+FLOPS = 2 * N * (P * H + H * H + H * H)
+
+BF16, F32, U16 = mybir.dt.bfloat16, mybir.dt.float32, mybir.dt.uint16
+RELU = mybir.ActivationFunctionType.Relu
+ADD, MAX = mybir.AluOpType.add, mybir.AluOpType.max
+
+
+def tile_safnn_kernel(tc, table, w0, b0, w1, b1, w2, b2, offs, out):
+    nc = tc.nc
+    with (
+        tc.tile_pool(name="held", bufs=1) as held,
+        tc.tile_pool(name="wide", bufs=LAYERS * BLOCKS * PIECES) as wide,
+        tc.tile_pool(name="narrow", bufs=(LAYERS - 1) * BLOCKS * PIECES) as narrow,
+        tc.psum_pool(name="psum", bufs=8) as psum,
+    ):
+        offsets = held.tile([P, N // 16], U16, name="offsets")
+        nc.sync.dma_start(offsets[:], offs)
+        table_sb = held.tile([P, S], BF16, name="table_sb")
+        nc.sync.dma_start(table_sb[:], table)
+
+        w0_sb = held.tile([P, H], BF16, name="w0_sb")
+        nc.scalar.dma_start(w0_sb[:], w0)
+        w1_sb = held.tile([P, BLOCKS, H], BF16, name="w1_sb")
+        nc.scalar.dma_start(w1_sb[:], w1.rearrange("(k p) m -> p k m", p=P))
+        w2_sb = held.tile([P, BLOCKS, H], BF16, name="w2_sb")
+        nc.scalar.dma_start(w2_sb[:], w2.rearrange("(k p) m -> p k m", p=P))
+        hidden_weights = {1: w1_sb, 2: w2_sb}
+
+        biases = []
+        with nc.allow_non_contiguous_dma(reason="a bias has one float32 for each partition"):
+            for layer, b in enumerate((b0, b1, b2)):
+                b_sb = held.tile([P, BLOCKS], F32, name=f"b{layer}_sb")
+                nc.gpsimd.dma_start(b_sb[:], b.rearrange("(m p) o -> p (m o)", p=P))
+                biases.append(b_sb)
+
+        previous = {}
+        for layer in range(LAYERS):
+            current = {}
+            for piece in range(PIECES):
+                for m in range(BLOCKS):
+                    features = slice(m * P, (m + 1) * P)
+                    acc = psum.tile([P, PIECE], F32, name="acc")
+                    if layer == 0:
+                        piece_offsets = offsets[:, piece * (PIECE // 16) : (piece + 1) * (PIECE // 16)]
+                        nc.tensor.matmul(
+                            acc[:], w0_sb[:, features], table_sb[:].indirect(piece_offsets), start=True, stop=True
+                        )
+                    else:
+                        for k in range(BLOCKS):
+                            nc.tensor.matmul(
+                                acc[:],
+                                hidden_weights[layer][:, k, features],
+                                previous[piece, k][:],
+                                start=(k == 0),
+                                stop=(k == BLOCKS - 1),
+                            )
+
+                    bias = biases[layer][:, m : m + 1]
+                    h_f32 = wide.tile([P, PIECE], F32, name="h_f32")
+                    if m % 2 == 0:
+                        nc.scalar.activation(h_f32[:], acc[:], RELU, bias=bias)
+                    else:
+                        nc.vector.tensor_scalar(h_f32[:], acc[:], bias, 0.0, ADD, MAX)
+
+                    if layer < LAYERS - 1:
+                        h_bf16 = narrow.tile([P, PIECE], BF16, name="h_bf16")
+                        nc.vector.tensor_copy(h_bf16[:], h_f32[:])
+                        current[piece, m] = h_bf16
+
+                    rows = slice((layer * BLOCKS + m) * P, (layer * BLOCKS + m + 1) * P)
+                    nc.sync.dma_start(out[rows, piece * PIECE : (piece + 1) * PIECE], h_f32[:])
+            previous = current

@@ -8,6 +8,7 @@ LAYERS = 3
 BLOCKS = H // P
 PIECE = 512
 PIECES = N // PIECE
+WARM_MATMULS = 4
 FLOPS = 2 * N * (P * H + H * H + H * H)
 
 BF16, F32, U16 = mybir.dt.bfloat16, mybir.dt.float32, mybir.dt.uint16
@@ -21,27 +22,33 @@ def tile_safnn_kernel(tc, table, w0, b0, w1, b1, w2, b2, offs, out):
         tc.tile_pool(name="held", bufs=1) as held,
         tc.tile_pool(name="wide", bufs=LAYERS * BLOCKS * PIECES) as wide,
         tc.tile_pool(name="narrow", bufs=(LAYERS - 1) * BLOCKS * PIECES) as narrow,
-        tc.psum_pool(name="psum", bufs=8) as psum,
+        tc.psum_pool(name="psum", bufs=7) as psum,
+        tc.psum_pool(name="idle", bufs=1) as idle,
     ):
+        zeros = held.tile([P, PIECE], BF16, name="zeros")
+        nc.vector.memset(zeros[:], 0.0)
+        early_relu = held.tile([P, 1], BF16, name="early_relu")
+        nc.scalar.activation(early_relu[:], zeros[:, :1], RELU)
+        unused = idle.tile([P, PIECE], F32, name="unused")
+        for i in range(WARM_MATMULS):
+            nc.tensor.matmul(unused[:], zeros[:, :P], zeros[:], start=True, stop=True)
+
         offsets = held.tile([P, N // 16], U16, name="offsets")
         nc.sync.dma_start(offsets[:], offs)
         table_sb = held.tile([P, S], BF16, name="table_sb")
         nc.sync.dma_start(table_sb[:], table)
 
         w0_sb = held.tile([P, H], BF16, name="w0_sb")
-        nc.scalar.dma_start(w0_sb[:], w0)
         w1_sb = held.tile([P, BLOCKS, H], BF16, name="w1_sb")
-        nc.scalar.dma_start(w1_sb[:], w1.rearrange("(k p) m -> p k m", p=P))
         w2_sb = held.tile([P, BLOCKS, H], BF16, name="w2_sb")
-        nc.scalar.dma_start(w2_sb[:], w2.rearrange("(k p) m -> p k m", p=P))
         hidden_weights = {1: w1_sb, 2: w2_sb}
-
-        biases = []
+        biases = [held.tile([P, BLOCKS], F32, name=f"b{layer}_sb") for layer in range(LAYERS)]
         with nc.allow_non_contiguous_dma(reason="a bias has one float32 for each partition"):
-            for layer, b in enumerate((b0, b1, b2)):
-                b_sb = held.tile([P, BLOCKS], F32, name=f"b{layer}_sb")
-                nc.gpsimd.dma_start(b_sb[:], b.rearrange("(m p) o -> p (m o)", p=P))
-                biases.append(b_sb)
+            nc.scalar.dma_start(w0_sb[:], w0)
+            for b_sb, b in zip(biases, (b0, b1, b2)):
+                nc.scalar.dma_start(b_sb[:], b.rearrange("(m p) o -> p (m o)", p=P))
+        nc.sync.dma_start(w1_sb[:], w1.rearrange("(k p) m -> p k m", p=P))
+        nc.sync.dma_start(w2_sb[:], w2.rearrange("(k p) m -> p k m", p=P))
 
         previous = {}
         for layer in range(LAYERS):
@@ -67,15 +74,17 @@ def tile_safnn_kernel(tc, table, w0, b0, w1, b1, w2, b2, offs, out):
 
                     bias = biases[layer][:, m : m + 1]
                     h_f32 = wide.tile([P, PIECE], F32, name="h_f32")
-                    if m % 2 == 0:
-                        nc.scalar.activation(h_f32[:], acc[:], RELU, bias=bias)
-                    else:
-                        nc.vector.tensor_scalar(h_f32[:], acc[:], bias, 0.0, ADD, MAX)
-
                     if layer < LAYERS - 1:
                         h_bf16 = narrow.tile([P, PIECE], BF16, name="h_bf16")
-                        nc.vector.tensor_copy(h_bf16[:], h_f32[:])
                         current[piece, m] = h_bf16
+                    if m % 2 == 0:
+                        nc.vector.tensor_scalar(h_f32[:], acc[:], bias, 0.0, ADD, MAX)
+                        if layer < LAYERS - 1:
+                            nc.vector.tensor_copy(h_bf16[:], h_f32[:])
+                    else:
+                        if layer < LAYERS - 1:
+                            nc.scalar.activation(h_bf16[:], acc[:], RELU, bias=bias)
+                        nc.scalar.activation(h_f32[:], acc[:], RELU, bias=bias)
 
                     rows = slice((layer * BLOCKS + m) * P, (layer * BLOCKS + m + 1) * P)
                     nc.sync.dma_start(out[rows, piece * PIECE : (piece + 1) * PIECE], h_f32[:])

@@ -45,10 +45,11 @@ def tile_safnn_kernel(tc, table, w0, b0, w1, b1, w2, b2, offs, out):
         biases = [held.tile([P, BLOCKS], F32, name=f"b{layer}_sb") for layer in range(LAYERS)]
         with nc.allow_non_contiguous_dma(reason="a bias has one float32 for each partition"):
             nc.scalar.dma_start(w0_sb[:], w0)
-            for b_sb, b in zip(biases, (b0, b1, b2)):
-                nc.scalar.dma_start(b_sb[:], b.rearrange("(m p) o -> p (m o)", p=P))
-        nc.sync.dma_start(w1_sb[:], w1.rearrange("(k p) m -> p k m", p=P))
-        nc.sync.dma_start(w2_sb[:], w2.rearrange("(k p) m -> p k m", p=P))
+            nc.scalar.dma_start(biases[0][:], b0.rearrange("(m p) o -> p (m o)", p=P))
+            nc.sync.dma_start(w1_sb[:], w1.rearrange("(k p) m -> p k m", p=P))
+            nc.sync.dma_start(biases[1][:], b1.rearrange("(m p) o -> p (m o)", p=P))
+            nc.sync.dma_start(w2_sb[:], w2.rearrange("(k p) m -> p k m", p=P))
+            nc.sync.dma_start(biases[2][:], b2.rearrange("(m p) o -> p (m o)", p=P))
 
         previous = {}
         for layer in range(LAYERS):

@@ -6,8 +6,10 @@ H = 256
 N = 1024
 LAYERS = 3
 BLOCKS = H // P
-PIECE = 512
+BANK = 512
+PIECE = 256
 PIECES = N // PIECE
+STORED = 2
 WARM_MATMULS = 4
 FLOPS = 2 * N * (P * H + H * H + H * H)
 
@@ -20,16 +22,16 @@ def tile_safnn_kernel(tc, table, w0, b0, w1, b1, w2, b2, offs, out):
     nc = tc.nc
     with (
         tc.tile_pool(name="held", bufs=1) as held,
-        tc.tile_pool(name="wide", bufs=LAYERS * BLOCKS * PIECES) as wide,
+        tc.tile_pool(name="wide", bufs=LAYERS * BLOCKS * PIECES // STORED) as wide,
         tc.tile_pool(name="narrow", bufs=(LAYERS - 1) * BLOCKS * PIECES) as narrow,
         tc.psum_pool(name="psum", bufs=7) as psum,
         tc.psum_pool(name="idle", bufs=1) as idle,
     ):
-        zeros = held.tile([P, PIECE], BF16, name="zeros")
+        zeros = held.tile([P, BANK], BF16, name="zeros")
         nc.vector.memset(zeros[:], 0.0)
         early_relu = held.tile([P, 1], BF16, name="early_relu")
         nc.scalar.activation(early_relu[:], zeros[:, :1], RELU)
-        unused = idle.tile([P, PIECE], F32, name="unused")
+        unused = idle.tile([P, BANK], F32, name="unused")
         for i in range(WARM_MATMULS):
             nc.tensor.matmul(unused[:], zeros[:, :P], zeros[:], start=True, stop=True)
 
@@ -54,6 +56,7 @@ def tile_safnn_kernel(tc, table, w0, b0, w1, b1, w2, b2, offs, out):
         previous = {}
         for layer in range(LAYERS):
             current = {}
+            staged = {}
             for piece in range(PIECES):
                 for m in range(BLOCKS):
                     features = slice(m * P, (m + 1) * P)
@@ -74,19 +77,23 @@ def tile_safnn_kernel(tc, table, w0, b0, w1, b1, w2, b2, offs, out):
                             )
 
                     bias = biases[layer][:, m : m + 1]
-                    h_f32 = wide.tile([P, PIECE], F32, name="h_f32")
+                    place = piece % STORED
+                    if place == 0:
+                        staged[m] = wide.tile([P, STORED * PIECE], F32, name="staged")
+                    h_f32 = staged[m][:, place * PIECE : (place + 1) * PIECE]
                     if layer < LAYERS - 1:
                         h_bf16 = narrow.tile([P, PIECE], BF16, name="h_bf16")
                         current[piece, m] = h_bf16
                     if m % 2 == 0:
-                        nc.vector.tensor_scalar(h_f32[:], acc[:], bias, 0.0, ADD, MAX)
+                        nc.vector.tensor_scalar(h_f32, acc[:], bias, 0.0, ADD, MAX)
                         if layer < LAYERS - 1:
-                            nc.vector.tensor_copy(h_bf16[:], h_f32[:])
+                            nc.vector.tensor_copy(h_bf16[:], h_f32)
                     else:
                         if layer < LAYERS - 1:
                             nc.scalar.activation(h_bf16[:], acc[:], RELU, bias=bias)
-                        nc.scalar.activation(h_f32[:], acc[:], RELU, bias=bias)
+                        nc.scalar.activation(h_f32, acc[:], RELU, bias=bias)
 
-                    rows = slice((layer * BLOCKS + m) * P, (layer * BLOCKS + m + 1) * P)
-                    nc.sync.dma_start(out[rows, piece * PIECE : (piece + 1) * PIECE], h_f32[:])
+                    if place == STORED - 1:
+                        rows = slice((layer * BLOCKS + m) * P, (layer * BLOCKS + m + 1) * P)
+                        nc.sync.dma_start(out[rows, (piece + 1 - STORED) * PIECE : (piece + 1) * PIECE], staged[m][:])
             previous = current

@@ -89,9 +89,9 @@ def tile_safnn_kernel(tc, table, w0, b0, w1, b1, w2, b2, offs, out):
                         if layer < LAYERS - 1:
                             nc.vector.tensor_copy(h_bf16[:], h_f32)
                     else:
+                        nc.scalar.activation(h_f32, acc[:], RELU, bias=bias)
                         if layer < LAYERS - 1:
                             nc.scalar.activation(h_bf16[:], acc[:], RELU, bias=bias)
-                        nc.scalar.activation(h_f32, acc[:], RELU, bias=bias)
 
                     if place == STORED - 1:
                         rows = slice((layer * BLOCKS + m) * P, (layer * BLOCKS + m + 1) * P)

@@ -77,21 +77,20 @@ def tile_safnn_kernel(tc, table, w0, b0, w1, b1, w2, b2, offs, out):
                             )
 
                     bias = biases[layer][:, m : m + 1]
+                    feeds_next = layer < LAYERS - 1
                     place = piece % STORED
                     if place == 0:
                         staged[m] = wide.tile([P, STORED * PIECE], F32, name="staged")
                     h_f32 = staged[m][:, place * PIECE : (place + 1) * PIECE]
-                    if layer < LAYERS - 1:
-                        h_bf16 = narrow.tile([P, PIECE], BF16, name="h_bf16")
-                        current[piece, m] = h_bf16
-                    if m % 2 == 0:
+                    bank_number = piece * BLOCKS + m
+                    if bank_number % (4 if feeds_next else 2) == 0:
                         nc.vector.tensor_scalar(h_f32, acc[:], bias, 0.0, ADD, MAX)
-                        if layer < LAYERS - 1:
-                            nc.vector.tensor_copy(h_bf16[:], h_f32)
                     else:
                         nc.scalar.activation(h_f32, acc[:], RELU, bias=bias)
-                        if layer < LAYERS - 1:
-                            nc.scalar.activation(h_bf16[:], acc[:], RELU, bias=bias)
+                    if feeds_next:
+                        h_bf16 = narrow.tile([P, PIECE], BF16, name="h_bf16")
+                        current[piece, m] = h_bf16
+                        nc.vector.tensor_copy(h_bf16[:], h_f32)
 
                     if place == STORED - 1:
                         rows = slice((layer * BLOCKS + m) * P, (layer * BLOCKS + m + 1) * P)

@@ -6,11 +6,9 @@ H = 256
 N = 1024
 LAYERS = 3
 BLOCKS = H // P
-BANK = 512
 PIECE = 256
 PIECES = N // PIECE
 STORED = 2
-WARM_MATMULS = 4
 FLOPS = 2 * N * (P * H + H * H + H * H)
 
 BF16, F32, U16 = mybir.dt.bfloat16, mybir.dt.float32, mybir.dt.uint16
@@ -24,16 +22,12 @@ def tile_safnn_kernel(tc, table, w0, b0, w1, b1, w2, b2, offs, out):
         tc.tile_pool(name="held", bufs=1) as held,
         tc.tile_pool(name="wide", bufs=LAYERS * BLOCKS * PIECES // STORED) as wide,
         tc.tile_pool(name="narrow", bufs=(LAYERS - 1) * BLOCKS * PIECES) as narrow,
-        tc.psum_pool(name="psum", bufs=7) as psum,
-        tc.psum_pool(name="idle", bufs=1) as idle,
+        tc.psum_pool(name="psum", bufs=8) as psum,
     ):
-        zeros = held.tile([P, BANK], BF16, name="zeros")
-        nc.vector.memset(zeros[:], 0.0)
+        zero = held.tile([P, 1], BF16, name="zero")
+        nc.vector.memset(zero[:], 0.0)
         early_relu = held.tile([P, 1], BF16, name="early_relu")
-        nc.scalar.activation(early_relu[:], zeros[:, :1], RELU)
-        unused = idle.tile([P, BANK], F32, name="unused")
-        for i in range(WARM_MATMULS):
-            nc.tensor.matmul(unused[:], zeros[:, :P], zeros[:], start=True, stop=True)
+        nc.scalar.activation(early_relu[:], zero[:], RELU)
 
         offsets = held.tile([P, N // 16], U16, name="offsets")
         nc.sync.dma_start(offsets[:], offs)

@@ -49,44 +49,43 @@ def tile_safnn_kernel(tc, table, w0, b0, w1, b1, w2, b2, offs, out):
 
         previous = {}
         for layer in range(LAYERS):
+            feeds_next = layer < LAYERS - 1
             current = {}
-            staged = {}
-            for piece in range(PIECES):
+            banks_used = 0
+            for first_piece in range(0, PIECES, STORED):
                 for m in range(BLOCKS):
                     features = slice(m * P, (m + 1) * P)
-                    acc = psum.tile([P, PIECE], F32, name="acc")
-                    if layer == 0:
-                        piece_offsets = offsets[:, piece * (PIECE // 16) : (piece + 1) * (PIECE // 16)]
-                        nc.tensor.matmul(
-                            acc[:], w0_sb[:, features], table_sb[:].indirect(piece_offsets), start=True, stop=True
-                        )
-                    else:
-                        for k in range(BLOCKS):
-                            nc.tensor.matmul(
-                                acc[:],
-                                hidden_weights[layer][:, k, features],
-                                previous[piece, k][:],
-                                start=(k == 0),
-                                stop=(k == BLOCKS - 1),
-                            )
-
                     bias = biases[layer][:, m : m + 1]
-                    feeds_next = layer < LAYERS - 1
-                    place = piece % STORED
-                    if place == 0:
-                        staged[m] = wide.tile([P, STORED * PIECE], F32, name="staged")
-                    h_f32 = staged[m][:, place * PIECE : (place + 1) * PIECE]
-                    bank_number = piece * BLOCKS + m
-                    if bank_number % (4 if feeds_next else 2) == 0:
-                        nc.vector.tensor_scalar(h_f32, acc[:], bias, 0.0, ADD, MAX)
-                    else:
-                        nc.scalar.activation(h_f32, acc[:], RELU, bias=bias)
-                    if feeds_next:
-                        h_bf16 = narrow.tile([P, PIECE], BF16, name="h_bf16")
-                        current[piece, m] = h_bf16
-                        nc.vector.tensor_copy(h_bf16[:], h_f32)
+                    staged = wide.tile([P, STORED * PIECE], F32, name="staged")
+                    for place in range(STORED):
+                        piece = first_piece + place
+                        acc = psum.tile([P, PIECE], F32, name="acc")
+                        if layer == 0:
+                            piece_offsets = offsets[:, piece * (PIECE // 16) : (piece + 1) * (PIECE // 16)]
+                            nc.tensor.matmul(
+                                acc[:], w0_sb[:, features], table_sb[:].indirect(piece_offsets), start=True, stop=True
+                            )
+                        else:
+                            for k in range(BLOCKS):
+                                nc.tensor.matmul(
+                                    acc[:],
+                                    hidden_weights[layer][:, k, features],
+                                    previous[piece, k][:],
+                                    start=(k == 0),
+                                    stop=(k == BLOCKS - 1),
+                                )
 
-                    if place == STORED - 1:
-                        rows = slice((layer * BLOCKS + m) * P, (layer * BLOCKS + m + 1) * P)
-                        nc.sync.dma_start(out[rows, (piece + 1 - STORED) * PIECE : (piece + 1) * PIECE], staged[m][:])
+                        h_f32 = staged[:, place * PIECE : (place + 1) * PIECE]
+                        if banks_used % (4 if feeds_next else 2) == 0:
+                            nc.vector.tensor_scalar(h_f32, acc[:], bias, 0.0, ADD, MAX)
+                        else:
+                            nc.scalar.activation(h_f32, acc[:], RELU, bias=bias)
+                        banks_used += 1
+                        if feeds_next:
+                            h_bf16 = narrow.tile([P, PIECE], BF16, name="h_bf16")
+                            current[piece, m] = h_bf16
+                            nc.vector.tensor_copy(h_bf16[:], h_f32)
+
+                    rows = slice((layer * BLOCKS + m) * P, (layer * BLOCKS + m + 1) * P)
+                    nc.sync.dma_start(out[rows, first_piece * PIECE : (first_piece + STORED) * PIECE], staged[:])
             previous = current

@@ -24,11 +24,6 @@ def tile_safnn_kernel(tc, table, w0, b0, w1, b1, w2, b2, offs, out):
         tc.tile_pool(name="narrow", bufs=(LAYERS - 1) * BLOCKS * PIECES) as narrow,
         tc.psum_pool(name="psum", bufs=8) as psum,
     ):
-        zero = held.tile([P, 1], BF16, name="zero")
-        nc.vector.memset(zero[:], 0.0)
-        early_relu = held.tile([P, 1], BF16, name="early_relu")
-        nc.scalar.activation(early_relu[:], zero[:], RELU)
-
         offsets = held.tile([P, N // 16], U16, name="offsets")
         nc.sync.dma_start(offsets[:], offs)
         table_sb = held.tile([P, S], BF16, name="table_sb")
@@ -46,6 +41,11 @@ def tile_safnn_kernel(tc, table, w0, b0, w1, b1, w2, b2, offs, out):
             nc.sync.dma_start(biases[1][:], b1.rearrange("(m p) o -> p (m o)", p=P))
             nc.sync.dma_start(w2_sb[:], w2.rearrange("(k p) m -> p k m", p=P))
             nc.sync.dma_start(biases[2][:], b2.rearrange("(m p) o -> p (m o)", p=P))
+
+        zero = held.tile([P, 1], BF16, name="zero")
+        nc.vector.memset(zero[:], 0.0)
+        early_relu = held.tile([P, 1], BF16, name="early_relu")
+        nc.scalar.activation(early_relu[:], zero[:], RELU)
 
         previous = {}
         for layer in range(LAYERS):

@@ -27,7 +27,7 @@ def tile_safnn_kernel(tc, table, w0, b0, w1, b1, w2, b2, offs, out):
         offsets = held.tile([P, N // 16], U16, name="offsets")
         nc.sync.dma_start(offsets[:], offs)
         table_sb = held.tile([P, S], BF16, name="table_sb")
-        nc.sync.dma_start(table_sb[:], table)
+        nc.scalar.dma_start(table_sb[:], table)
 
         w0_sb = held.tile([P, H], BF16, name="w0_sb")
         w1_sb = held.tile([P, BLOCKS, H], BF16, name="w1_sb")
@@ -35,8 +35,8 @@ def tile_safnn_kernel(tc, table, w0, b0, w1, b1, w2, b2, offs, out):
         hidden_weights = {1: w1_sb, 2: w2_sb}
         biases = [held.tile([P, BLOCKS], F32, name=f"b{layer}_sb") for layer in range(LAYERS)]
         with nc.allow_non_contiguous_dma(reason="a bias has one float32 for each partition"):
-            nc.scalar.dma_start(w0_sb[:], w0)
-            nc.scalar.dma_start(biases[0][:], b0.rearrange("(m p) o -> p (m o)", p=P))
+            nc.sync.dma_start(w0_sb[:], w0)
+            nc.sync.dma_start(biases[0][:], b0.rearrange("(m p) o -> p (m o)", p=P))
             nc.sync.dma_start(w1_sb[:], w1.rearrange("(k p) m -> p k m", p=P))
             nc.sync.dma_start(biases[1][:], b1.rearrange("(m p) o -> p (m o)", p=P))
             nc.sync.dma_start(w2_sb[:], w2.rearrange("(k p) m -> p k m", p=P))

@@ -9,6 +9,7 @@ BLOCKS = H // P
 PIECE = 256
 PIECES = N // PIECE
 STORED = 2
+LINE = 256
 FLOPS = 2 * N * (P * H + H * H + H * H)
 
 BF16, F32, U16 = mybir.dt.bfloat16, mybir.dt.float32, mybir.dt.uint16
@@ -26,12 +27,12 @@ def tile_safnn_kernel(tc, table, w0, b0, w1, b1, w2, b2, offs, out):
     ):
         offsets = held.tile([P, N // 16], U16, name="offsets")
         nc.sync.dma_start(offsets[:], offs)
-        table_sb = held.tile([P, S], BF16, name="table_sb")
+        table_sb = held.tile([P, S], BF16, name="table_sb", align_bytes=LINE)
         nc.scalar.dma_start(table_sb[:], table)
 
-        w0_sb = held.tile([P, H], BF16, name="w0_sb")
-        w1_sb = held.tile([P, BLOCKS, H], BF16, name="w1_sb")
-        w2_sb = held.tile([P, BLOCKS, H], BF16, name="w2_sb")
+        w0_sb = held.tile([P, H], BF16, name="w0_sb", align_bytes=LINE)
+        w1_sb = held.tile([P, BLOCKS, H], BF16, name="w1_sb", align_bytes=LINE)
+        w2_sb = held.tile([P, BLOCKS, H], BF16, name="w2_sb", align_bytes=LINE)
         hidden_weights = {1: w1_sb, 2: w2_sb}
         biases = [held.tile([P, BLOCKS], F32, name=f"b{layer}_sb") for layer in range(LAYERS)]
         with nc.allow_non_contiguous_dma(reason="a bias has one float32 for each partition"):
@@ -56,7 +57,7 @@ def tile_safnn_kernel(tc, table, w0, b0, w1, b1, w2, b2, offs, out):
                 for m in range(BLOCKS):
                     features = slice(m * P, (m + 1) * P)
                     bias = biases[layer][:, m : m + 1]
-                    staged = wide.tile([P, STORED * PIECE], F32, name="staged")
+                    staged = wide.tile([P, STORED * PIECE], F32, name="staged", align_bytes=LINE)
                     for place in range(STORED):
                         piece = first_piece + place
                         acc = psum.tile([P, PIECE], F32, name="acc")

@@ -37,11 +37,11 @@ def tile_safnn_kernel(tc, table, w0, b0, w1, b1, w2, b2, offs, out):
         biases = [held.tile([P, BLOCKS], F32, name=f"b{layer}_sb") for layer in range(LAYERS)]
         with nc.allow_non_contiguous_dma(reason="a bias has one float32 for each partition"):
             nc.sync.dma_start(w0_sb[:], w0)
-            nc.sync.dma_start(biases[0][:], b0.rearrange("(m p) o -> p (m o)", p=P))
-            nc.sync.dma_start(w1_sb[:], w1.rearrange("(k p) m -> p k m", p=P))
-            nc.sync.dma_start(biases[1][:], b1.rearrange("(m p) o -> p (m o)", p=P))
-            nc.sync.dma_start(w2_sb[:], w2.rearrange("(k p) m -> p k m", p=P))
-            nc.sync.dma_start(biases[2][:], b2.rearrange("(m p) o -> p (m o)", p=P))
+            nc.scalar.dma_start(biases[0][:], b0.rearrange("(m p) o -> p (m o)", p=P))
+            nc.gpsimd.dma_start(w1_sb[:], w1.rearrange("(k p) m -> p k m", p=P))
+            nc.gpsimd.dma_start(biases[1][:], b1.rearrange("(m p) o -> p (m o)", p=P))
+            nc.gpsimd.dma_start(w2_sb[:], w2.rearrange("(k p) m -> p k m", p=P))
+            nc.gpsimd.dma_start(biases[2][:], b2.rearrange("(m p) o -> p (m o)", p=P))
 
         zero = held.tile([P, 1], BF16, name="zero")
         nc.vector.memset(zero[:], 0.0)

@@ -58,24 +58,28 @@ def tile_safnn_kernel(tc, table, w0, b0, w1, b1, w2, b2, offs, out):
                     features = slice(m * P, (m + 1) * P)
                     bias = biases[layer][:, m : m + 1]
                     staged = wide.tile([P, STORED * PIECE], F32, name="staged", align_bytes=LINE)
-                    for place in range(STORED):
-                        piece = first_piece + place
-                        acc = psum.tile([P, PIECE], F32, name="acc")
-                        if layer == 0:
+                    accs = [psum.tile([P, PIECE], F32, name="acc") for i in range(STORED)]
+                    if layer == 0:
+                        for place in range(STORED):
+                            piece = first_piece + place
                             piece_offsets = offsets[:, piece * (PIECE // 16) : (piece + 1) * (PIECE // 16)]
                             nc.tensor.matmul(
-                                acc[:], w0_sb[:, features], table_sb[:].indirect(piece_offsets), start=True, stop=True
+                                accs[place][:], w0_sb[:, features], table_sb[:].indirect(piece_offsets), start=True, stop=True
                             )
-                        else:
-                            for k in range(BLOCKS):
+                    else:
+                        for k in range(BLOCKS):
+                            for place in range(STORED):
                                 nc.tensor.matmul(
-                                    acc[:],
+                                    accs[place][:],
                                     hidden_weights[layer][:, k, features],
-                                    previous[piece, k][:],
+                                    previous[first_piece + place, k][:],
                                     start=(k == 0),
                                     stop=(k == BLOCKS - 1),
                                 )
 
+                    for place in range(STORED):
+                        piece = first_piece + place
+                        acc = accs[place]
                         h_f32 = staged[:, place * PIECE : (place + 1) * PIECE]
                         if banks_used % (4 if feeds_next else 2) == 0:
                             nc.vector.tensor_scalar(h_f32, acc[:], bias, 0.0, ADD, MAX)

@@ -35,19 +35,19 @@ def tile_safnn_kernel(tc, table, w0, b0, w1, b1, w2, b2, offs, out):
         w2_sb = held.tile([P, BLOCKS, H], BF16, name="w2_sb", align_bytes=LINE)
         hidden_weights = {1: w1_sb, 2: w2_sb}
         biases = [held.tile([P, BLOCKS], F32, name=f"b{layer}_sb") for layer in range(LAYERS)]
-        with nc.allow_non_contiguous_dma(reason="a bias has one float32 for each partition"):
-            nc.sync.dma_start(w0_sb[:], w0)
-            nc.scalar.dma_start(biases[0][:], b0.rearrange("(m p) o -> p (m o)", p=P))
-            nc.gpsimd.dma_start(w1_sb[:], w1.rearrange("(k p) m -> p k m", p=P))
-            nc.gpsimd.dma_start(biases[1][:], b1.rearrange("(m p) o -> p (m o)", p=P))
-            nc.gpsimd.dma_start(w2_sb[:], w2.rearrange("(k p) m -> p k m", p=P))
-            nc.gpsimd.dma_start(biases[2][:], b2.rearrange("(m p) o -> p (m o)", p=P))
+        nc.sync.dma_start(w0_sb[:], w0)
+        nc.scalar.dma_start(biases[0][:], b0.rearrange("(p m) o -> p (m o)", p=P))
+        nc.gpsimd.dma_start(w1_sb[:], w1.rearrange("(p k) m -> p k m", p=P))
+        nc.gpsimd.dma_start(biases[1][:], b1.rearrange("(p m) o -> p (m o)", p=P))
+        nc.gpsimd.dma_start(w2_sb[:], w2.rearrange("(p k) m -> p k m", p=P))
+        nc.gpsimd.dma_start(biases[2][:], b2.rearrange("(p m) o -> p (m o)", p=P))
 
         zero = held.tile([P, 1], BF16, name="zero")
         nc.vector.memset(zero[:], 0.0)
         early_relu = held.tile([P, 1], BF16, name="early_relu")
         nc.scalar.activation(early_relu[:], zero[:], RELU)
 
+        out_by_block = out.rearrange("(l p m) n -> p l m n", l=LAYERS, p=P)
         previous = {}
         for layer in range(LAYERS):
             feeds_next = layer < LAYERS - 1
@@ -55,7 +55,6 @@ def tile_safnn_kernel(tc, table, w0, b0, w1, b1, w2, b2, offs, out):
             banks_used = 0
             for first_piece in range(0, PIECES, STORED):
                 for m in range(BLOCKS):
-                    features = slice(m * P, (m + 1) * P)
                     bias = biases[layer][:, m : m + 1]
                     staged = wide.tile([P, STORED * PIECE], F32, name="staged", align_bytes=LINE)
                     accs = [psum.tile([P, PIECE], F32, name="acc") for i in range(STORED)]
@@ -64,14 +63,14 @@ def tile_safnn_kernel(tc, table, w0, b0, w1, b1, w2, b2, offs, out):
                             piece = first_piece + place
                             piece_offsets = offsets[:, piece * (PIECE // 16) : (piece + 1) * (PIECE // 16)]
                             nc.tensor.matmul(
-                                accs[place][:], w0_sb[:, features], table_sb[:].indirect(piece_offsets), start=True, stop=True
+                                accs[place][:], w0_sb[:, m::BLOCKS], table_sb[:].indirect(piece_offsets), start=True, stop=True
                             )
                     else:
                         for k in range(BLOCKS):
                             for place in range(STORED):
                                 nc.tensor.matmul(
                                     accs[place][:],
-                                    hidden_weights[layer][:, k, features],
+                                    hidden_weights[layer][:, k, m::BLOCKS],
                                     previous[first_piece + place, k][:],
                                     start=(k == 0),
                                     stop=(k == BLOCKS - 1),
@@ -91,6 +90,6 @@ def tile_safnn_kernel(tc, table, w0, b0, w1, b1, w2, b2, offs, out):
                             current[piece, m] = h_bf16
                             nc.vector.tensor_copy(h_bf16[:], h_f32)
 
-                    rows = slice((layer * BLOCKS + m) * P, (layer * BLOCKS + m + 1) * P)
-                    nc.sync.dma_start(out[rows, first_piece * PIECE : (first_piece + STORED) * PIECE], staged[:])
+                    samples = slice(first_piece * PIECE, (first_piece + STORED) * PIECE)
+                    nc.sync.dma_start(out_by_block[:, layer, m, samples], staged[:])
             previous = current

import concourse.mybir as mybir

P = 128
S = 2048
H = 256
N = 1024
LAYERS = 3
BLOCKS = H // P
PIECE = 256
PIECES = N // PIECE
STORED = 2
LINE = 256
FLOPS = 2 * N * (P * H + H * H + H * H)

BF16, F32, U16 = mybir.dt.bfloat16, mybir.dt.float32, mybir.dt.uint16
RELU = mybir.ActivationFunctionType.Relu
ADD, MAX = mybir.AluOpType.add, mybir.AluOpType.max


def tile_safnn_kernel(tc, table, w0, b0, w1, b1, w2, b2, offs, out):
    nc = tc.nc
    with (
        tc.tile_pool(name="held", bufs=1) as held,
        tc.tile_pool(name="wide", bufs=LAYERS * BLOCKS * PIECES // STORED) as wide,
        tc.tile_pool(name="narrow", bufs=(LAYERS - 1) * BLOCKS * PIECES) as narrow,
        tc.psum_pool(name="psum", bufs=8) as psum,
    ):
        offsets = held.tile([P, N // 16], U16, name="offsets")
        nc.sync.dma_start(offsets[:], offs)
        table_sb = held.tile([P, S], BF16, name="table_sb", align_bytes=LINE)
        nc.scalar.dma_start(table_sb[:], table)

        w0_sb = held.tile([P, H], BF16, name="w0_sb", align_bytes=LINE)
        w1_sb = held.tile([P, BLOCKS, H], BF16, name="w1_sb", align_bytes=LINE)
        w2_sb = held.tile([P, BLOCKS, H], BF16, name="w2_sb", align_bytes=LINE)
        hidden_weights = {1: w1_sb, 2: w2_sb}
        biases = [held.tile([P, BLOCKS], F32, name=f"b{layer}_sb") for layer in range(LAYERS)]
        nc.sync.dma_start(w0_sb[:], w0)
        nc.scalar.dma_start(biases[0][:], b0.rearrange("(p m) o -> p (m o)", p=P))
        nc.gpsimd.dma_start(w1_sb[:], w1.rearrange("(p k) m -> p k m", p=P))
        nc.gpsimd.dma_start(biases[1][:], b1.rearrange("(p m) o -> p (m o)", p=P))
        nc.gpsimd.dma_start(w2_sb[:], w2.rearrange("(p k) m -> p k m", p=P))
        nc.gpsimd.dma_start(biases[2][:], b2.rearrange("(p m) o -> p (m o)", p=P))

        zero = held.tile([P, 1], BF16, name="zero")
        nc.vector.memset(zero[:], 0.0)
        early_relu = held.tile([P, 1], BF16, name="early_relu")
        nc.scalar.activation(early_relu[:], zero[:], RELU)

        out_by_block = out.rearrange("(l p m) n -> p l m n", l=LAYERS, p=P)
        previous = {}
        for layer in range(LAYERS):
            feeds_next = layer < LAYERS - 1
            current = {}
            banks_used = 0
            for first_piece in range(0, PIECES, STORED):
                for m in range(BLOCKS):
                    bias = biases[layer][:, m : m + 1]
                    staged = wide.tile([P, STORED * PIECE], F32, name="staged", align_bytes=LINE)
                    accs = [psum.tile([P, PIECE], F32, name="acc") for i in range(STORED)]
                    if layer == 0:
                        for place in range(STORED):
                            piece = first_piece + place
                            piece_offsets = offsets[:, piece * (PIECE // 16) : (piece + 1) * (PIECE // 16)]
                            nc.tensor.matmul(
                                accs[place][:], w0_sb[:, m::BLOCKS], table_sb[:].indirect(piece_offsets), start=True, stop=True
                            )
                    else:
                        for k in range(BLOCKS):
                            for place in range(STORED):
                                nc.tensor.matmul(
                                    accs[place][:],
                                    hidden_weights[layer][:, k, m::BLOCKS],
                                    previous[first_piece + place, k][:],
                                    start=(k == 0),
                                    stop=(k == BLOCKS - 1),
                                )

                    for place in range(STORED):
                        piece = first_piece + place
                        acc = accs[place]
                        h_f32 = staged[:, place * PIECE : (place + 1) * PIECE]
                        if banks_used % (4 if feeds_next else 2) == 0:
                            nc.vector.tensor_scalar(h_f32, acc[:], bias, 0.0, ADD, MAX)
                        else:
                            nc.scalar.activation(h_f32, acc[:], RELU, bias=bias)
                        banks_used += 1
                        if feeds_next:
                            h_bf16 = narrow.tile([P, PIECE], BF16, name="h_bf16")
                            current[piece, m] = h_bf16
                            nc.vector.tensor_copy(h_bf16[:], h_f32)

                    samples = slice(first_piece * PIECE, (first_piece + STORED) * PIECE)
                    nc.sync.dma_start(out_by_block[:, layer, m, samples], staged[:])
            previous = current
